import numpy as np
import ml_dtypes


def mxq(x, axis, fmt="e4m3"):
    dtype, down = {"e4m3": (ml_dtypes.float8_e4m3fn, 7), "e5m2": (ml_dtypes.float8_e5m2, 14)}[fmt]
    v = np.moveaxis(np.asarray(x, np.float32).astype(ml_dtypes.bfloat16).astype(np.float64), axis, -1)
    blocks = v.reshape(v.shape[:-1] + (-1, 32))
    amax = np.abs(blocks).max(-1, keepdims=True)
    byte = np.maximum(np.where(amax > 0, np.frexp(amax)[1] - 1 + 127, 0) - down, 1)
    scale = np.exp2(byte - 127.0)
    codes = (blocks / scale).astype(np.float32).astype(dtype).astype(np.float64)
    return np.moveaxis((codes * scale).reshape(v.shape), -1, axis)


WIDE = False


def mx_kscale(k):
    if not WIDE:
        return np.ones(k)
    levels = np.array([10, -10, 5, -5, 0])
    a = np.random.permutation(np.resize(levels, k // 512 * 4)).reshape(k // 512, 4)
    idx = np.arange(k)
    return np.exp2(a[idx // 512, idx % 128 // 32])


BF16 = ml_dtypes.bfloat16


def bf(x):
    return np.asarray(x, np.float32).astype(BF16)


def f64(x):
    return np.asarray(x).astype(np.float64)


B, D, HH, WW, P, R = 4, 512, 64, 64, 128, 16

EPSILON = 1e-05
C = 1.0


def expmap0(u, c):
    sc = np.sqrt(c)
    norm = np.maximum(np.sqrt(np.sum(u * u, axis=-1, keepdims=True)), 1e-15)
    return np.tanh(sc * norm) * u / (sc * norm)


def asinh(v):
    a = np.abs(v)
    return np.sign(v) * np.where(a < 0.01, a - a ** 3 / 6.0, np.log(a + np.sqrt(a * a + 1.0)))


def draw(n, a, b, basis):
    return a * (np.random.standard_normal((n, R)) @ basis) / np.sqrt(R) + b * np.random.standard_normal((n, D)) / np.sqrt(D)


def setup_inputs():
    basis = np.random.standard_normal((R, D)) / np.sqrt(D)
    s = mx_kscale(D)
    sn = s / 2.0 ** np.round(0.5 * np.log2(np.mean(s * s)))
    z = np.moveaxis((draw(B * HH * WW, 0.8, 0.5, basis) * sn).reshape(B, HH, WW, D), -1, 1)
    p = expmap0(draw(P, 0.55, 0.3, basis) * sn, C)
    dirs = draw(P, 1.0, 0.4, basis)
    normals = dirs / np.sqrt(np.sum(dirs * dirs, axis=-1, keepdims=True)) * (1.0 + 0.1 * np.random.standard_normal((P, 1))) / sn
    return {"z": bf(np.ascontiguousarray(z)), "p": bf(p), "normals": bf(normals)}


def reference(z, p, normals):
    z, p, normals = f64(z), f64(p), f64(normals)
    c = C
    c_sqrt = np.sqrt(c)

    z = np.ascontiguousarray(np.moveaxis(expmap0(np.moveaxis(z, 1, -1), c), -1, 1))

    p_hat = -p
    zq = mxq(z, 1, "e4m3").reshape(B, D, HH * WW)
    p_dot_z = (mxq(p_hat, 1, "e4m3") @ zq).reshape(B, P, HH, WW)
    z_dot_w = (mxq(normals, 1, "e4m3") @ zq).reshape(B, P, HH, WW)

    z_norm = np.sum(z * z, axis=1, keepdims=True)
    p_norm = np.sum(p * p, axis=-1)[None, :, None, None]
    w_norm = np.sum(normals * normals, axis=-1)[None, :, None, None]
    p_dot_w = np.sum(p_hat * normals, axis=-1)[None, :, None, None]

    lambda_p_c = 2.0
    denom = np.maximum(1 + 2 * c * p_dot_z + c ** 2 * z_norm * p_norm, EPSILON)
    alpha = (1 + 2 * c * p_dot_z + c * z_norm) / denom
    beta = (1 - c * p_norm) / denom

    p_m_y_w = alpha * p_dot_w + beta * z_dot_w
    p_m_y_w_norm = alpha ** 2 * p_norm + 2 * alpha * beta * p_dot_z + beta ** 2 * z_norm

    arg = np.minimum(
        2 * c_sqrt * p_m_y_w / np.maximum((1 - c * p_m_y_w_norm) * w_norm, EPSILON),
        85.0,
    )
    logits = lambda_p_c * w_norm / c_sqrt * asinh(arg)
    return -logits

@@ -1,0 +1,228 @@
+from contextlib import ExitStack
+
+import concourse.mybir as mybir
+from concourse.masks import make_identity
+
+FLOPS = 2 * 2 * 128 * 512 * 4 * 4096
+
+F32 = mybir.dt.float32
+BF16 = mybir.dt.bfloat16
+U32 = mybir.dt.uint32
+U8 = mybir.dt.uint8
+FP8X4 = mybir.dt.float8_e4m3fn_x4
+ALU = mybir.AluOpType
+ACT = mybir.ActivationFunctionType
+AX = mybir.AxisListType
+
+P = 128
+PACK = 4
+BATCH = 4
+PIX = 4096
+SUB = 512
+HALF = 2048
+BLK = 128
+EPS = 1e-5
+CUT = 0.005
+RT2 = 2.0 ** 0.5
+XC = CUT / RT2
+TANH_XC = XC - XC ** 3 / 3.0 + 2.0 * XC ** 5 / 15.0
+
+
+def tile_hyperboliclayer_t_kernel(tc, z, p, normals, out):
+    nc = tc.nc
+    with ExitStack() as ctx:
+        const = ctx.enter_context(tc.tile_pool(name="const", bufs=1))
+        zpool = ctx.enter_context(tc.tile_pool(name="zpool", bufs=3))
+        ypool = ctx.enter_context(tc.tile_pool(name="ypool", bufs=3))
+        small = ctx.enter_context(tc.tile_pool(name="small", bufs=2))
+        ep1 = ctx.enter_context(tc.tile_pool(name="ep1", bufs=2))
+        ep2 = ctx.enter_context(tc.tile_pool(name="ep2", bufs=2))
+        ps_zt = ctx.enter_context(tc.psum_pool(name="ps_zt", bufs=2))
+        ps_fb = ctx.enter_context(tc.psum_pool(name="ps_fb", bufs=2))
+        ps_ep = ctx.enter_context(tc.psum_pool(name="ps_ep", bufs=1))
+
+        ident_bf = const.tile([P, P], BF16)
+        make_identity(nc, ident_bf[:])
+        ident_f = const.tile([P, P], F32)
+        make_identity(nc, ident_f[:])
+
+        p_sb = const.tile([P, 512], BF16)
+        nc.sync.dma_start(out=p_sb[:], in_=p)
+        n_sb = const.tile([P, 512], BF16)
+        nc.sync.dma_start(out=n_sb[:], in_=normals)
+
+        z_tiles = []
+
+        def load_z(r):
+            z_sb = zpool.tile([P, PACK, PIX], BF16, name="z_sb")
+            nc.sync.dma_start(out=z_sb[:], in_=z[r].rearrange("(q t) h w -> q t (h w)", t=PACK))
+            z_tiles.append(z_sb)
+
+        for r in range(3):
+            load_z(r)
+
+        junk_c = const.tile([P, 512], F32)
+        pp = const.tile([P, 1], F32)
+        nc.scalar.activation(out=junk_c[:], in_=p_sb[:], func=ACT.Square, accum_out=pp[:])
+        ww = const.tile([P, 1], F32)
+        nc.scalar.activation(out=junk_c[:], in_=n_sb[:], func=ACT.Square, accum_out=ww[:])
+        prod = const.tile([P, 512], F32)
+        nc.vector.tensor_tensor(out=prod[:], in0=p_sb[:], in1=n_sb[:], op=ALU.mult)
+        spn = const.tile([P, 1], F32)
+        nc.vector.reduce_sum(out=spn[:], in_=prod[:], axis=AX.X)
+        c_4pw = const.tile([P, 1], F32)
+        nc.vector.tensor_scalar(out=c_4pw[:], in0=spn[:], scalar1=-4.0, scalar2=None, op0=ALU.mult)
+        c_m2pw = const.tile([P, 1], F32)
+        nc.vector.tensor_scalar(out=c_m2pw[:], in0=spn[:], scalar1=2.0, scalar2=None, op0=ALU.mult)
+        c_2b = const.tile([P, 1], F32)
+        nc.vector.tensor_scalar(out=c_2b[:], in0=pp[:], scalar1=-2.0, scalar2=2.0, op0=ALU.mult, op1=ALU.add)
+        c_1pp = const.tile([P, 1], F32)
+        nc.vector.tensor_scalar(out=c_1pp[:], in0=pp[:], scalar1=1.0, scalar2=None, op0=ALU.add)
+        c_mpp = const.tile([P, 1], F32)
+        nc.vector.tensor_scalar(out=c_mpp[:], in0=pp[:], scalar1=-1.0, scalar2=None, op0=ALU.mult)
+        c_b = const.tile([P, 1], F32)
+        nc.vector.tensor_scalar(out=c_b[:], in0=pp[:], scalar1=-1.0, scalar2=1.0, op0=ALU.mult, op1=ALU.add)
+        c_1 = const.tile([P, 1], F32)
+        nc.vector.tensor_tensor(out=c_1[:], in0=c_b[:], in1=ww[:], op=ALU.mult)
+        c_i1 = const.tile([P, 1], F32)
+        nc.vector.reciprocal(out=c_i1[:], in_=c_1[:])
+        c_out = const.tile([P, 1], F32)
+        nc.vector.tensor_scalar(out=c_out[:], in0=ww[:], scalar1=-1.0 / TANH_XC, scalar2=None, op0=ALU.mult)
+
+        wg = const.tile([P, 2 * PACK, P], BF16)
+        nc.vector.tensor_scalar(
+            out=wg[:, 0:PACK, :], in0=p_sb[:].rearrange("c (q t) -> c t q", t=PACK),
+            scalar1=-1.0, scalar2=None, op0=ALU.mult,
+        )
+        nc.vector.tensor_copy(out=wg[:, PACK : 2 * PACK, :], in_=n_sb[:].rearrange("c (q t) -> c t q", t=PACK))
+        wt_ps = ps_zt.tile([P, 2 * PACK, P], BF16, tag="zt")
+        for j in range(2 * PACK):
+            nc.tensor.transpose(wt_ps[:, j, :], wg[:, j, :], ident_bf[:])
+        wgrp = const.tile([P, 2, P, PACK], BF16, align_bytes=64)
+        nc.vector.tensor_copy(out=wgrp[:], in_=wt_ps[:].rearrange("q (o t) c -> q o c t", o=2))
+        wcodes = const.tile([P, 2 * P], U32, align_bytes=64)
+        wscale = const.tile([P, 2 * P], U8, align_bytes=64)
+        nc.vector.quantize_mx(
+            out=wcodes[:].bitcast(FP8X4), scales=wscale[:], in_=wgrp[:].rearrange("q o c t -> q (o c t)")
+        )
+
+        def norms(r):
+            z_sb = z_tiles[r]
+            nblk = PIX // BLK
+            s = small.tile([P, nblk], F32, name="s")
+            for b2 in range(nblk // 2):
+                zt = ps_zt.tile([P, 2, PACK, P], BF16, tag="zt", name="zt")
+                for u in range(2):
+                    blk = 2 * b2 + u
+                    for t in range(PACK):
+                        nc.tensor.transpose(zt[:, u, t, :], z_sb[:, t, blk * BLK : (blk + 1) * BLK], ident_bf[:])
+                for u in range(2):
+                    blk = 2 * b2 + u
+                    junk = small.tile([P, PACK * P], BF16, name="junk")
+                    nc.scalar.activation(
+                        out=junk[:], in_=zt[:, u, :, :].rearrange("p t q -> p (t q)"), func=ACT.Square,
+                        accum_out=s[:, blk : blk + 1],
+                    )
+            n = small.tile([P, nblk], F32, name="n")
+            nc.scalar.activation(out=n[:], in_=s[:], func=ACT.Sqrt)
+            nc.vector.tensor_scalar_max(out=n[:], in0=n[:], scalar1=1e-15)
+            th = small.tile([P, nblk], F32, name="th")
+            nc.scalar.activation(out=th[:], in_=n[:], func=ACT.Tanh)
+            e = small.tile([P, nblk], F32, name="e")
+            nc.scalar.activation(out=e[:], in_=n[:], func=ACT.Exp, scale=-2.0)
+            rn = small.tile([P, nblk], F32, name="rn")
+            nc.vector.reciprocal(out=rn[:], in_=n[:])
+            f = small.tile([P, nblk], F32, name="f")
+            nc.vector.tensor_tensor(out=f[:], in0=th[:], in1=rn[:], op=ALU.mult)
+            d = small.tile([P, nblk], F32, name="d")
+            nc.vector.tensor_scalar(out=d[:], in0=e[:], scalar1=1.0, scalar2=None, op0=ALU.add)
+            rd = small.tile([P, nblk], F32, name="rd")
+            nc.vector.reciprocal(out=rd[:], in_=d[:])
+            g = small.tile([P, nblk], F32, name="g")
+            nc.vector.scalar_tensor_tensor(out=g[:], in0=e[:], scalar=4.0, in1=rd[:], op0=ALU.mult, op1=ALU.mult)
+            nc.vector.tensor_tensor(out=g[:], in0=g[:], in1=rd[:], op=ALU.mult)
+            h = small.tile([P, nblk], F32, name="h")
+            nc.vector.reciprocal(out=h[:], in_=g[:])
+            return f, g, h
+
+        def spread(dst, col_tile, first_blk):
+            for j in range(SUB // BLK):
+                b = first_blk + j
+                nc.tensor.transpose(
+                    dst[:, j * BLK : (j + 1) * BLK], col_tile[:, b : b + 1].to_broadcast([P, P]), ident_f[:]
+                )
+
+        def sub_tile(r, i, fgh, ta, tb):
+            f, g, h = fgh
+            z_sb = z_tiles[r]
+            cs = slice((i % 4) * SUB, (i % 4 + 1) * SUB)
+            fb = ps_fb.tile([P, SUB], F32, name="fb")
+            spread(fb, f, 4 * i)
+            yg = ypool.tile([P, SUB, PACK], BF16, align_bytes=64, name="yg")
+            nc.vector.tensor_tensor(
+                out=yg[:], in0=z_sb[:, :, i * SUB : (i + 1) * SUB].rearrange("p t w -> p w t"),
+                in1=fb[:].unsqueeze(2).to_broadcast([P, SUB, PACK]), op=ALU.mult,
+            )
+            codes = ypool.tile([P, SUB], U32, align_bytes=64, name="codes")
+            scale = ypool.tile([P, SUB], U8, align_bytes=64, name="scale")
+            nc.vector.quantize_mx(
+                out=codes[:].bitcast(FP8X4), scales=scale[:], in_=yg[:].rearrange("p w t -> p (w t)")
+            )
+            a_ps = ps_ep.tile([P, SUB], F32, name="a_ps")
+            nc.tensor.matmul_mx(
+                out=a_ps[:], lhsT=wcodes[:, 0:P].bitcast(FP8X4), lhsT_scale=wscale[:, 0:P],
+                rhs=codes[:].bitcast(FP8X4), rhs_scale=scale[:], start=True, stop=True,
+            )
+            w_ps = ps_ep.tile([P, SUB], F32, name="w_ps")
+            nc.tensor.matmul_mx(
+                out=w_ps[:], lhsT=wcodes[:, P : 2 * P].bitcast(FP8X4), lhsT_scale=wscale[:, P : 2 * P],
+                rhs=codes[:].bitcast(FP8X4), rhs_scale=scale[:], start=True, stop=True,
+            )
+            gb = ps_ep.tile([P, SUB], F32, name="gb")
+            spread(gb, g, 4 * i)
+            hb = ps_ep.tile([P, SUB], F32, name="hb")
+            spread(hb, h, 4 * i)
+            nc.scalar.activation(out=ta[:, cs], in_=a_ps[:], func=ACT.Identity, scale=c_4pw[:], bias=c_4pw[:])
+            nc.scalar.activation(out=tb[:, cs], in_=a_ps[:], func=ACT.Identity, scale=2.0, bias=c_1pp[:])
+            nc.vector.scalar_tensor_tensor(
+                out=ta[:, cs], in0=gb[:], scalar=c_m2pw[:], in1=ta[:, cs], op0=ALU.mult, op1=ALU.add)
+            nc.vector.scalar_tensor_tensor(
+                out=ta[:, cs], in0=w_ps[:], scalar=c_2b[:], in1=ta[:, cs], op0=ALU.mult, op1=ALU.add)
+            nc.vector.scalar_tensor_tensor(
+                out=tb[:, cs], in0=gb[:], scalar=c_mpp[:], in1=tb[:, cs], op0=ALU.mult, op1=ALU.add)
+            nc.scalar.activation(out=tb[:, cs], in_=tb[:, cs], func=ACT.Abs_reciprocal_sqrt, scale=EPS)
+            nc.scalar.activation(out=tb[:, cs], in_=tb[:, cs], func=ACT.Square)
+            nc.vector.scalar_tensor_tensor(
+                out=tb[:, cs], in0=hb[:], scalar=c_i1[:], in1=tb[:, cs], op0=ALU.mult, op1=ALU.min)
+            nc.vector.tensor_tensor(out=ta[:, cs], in0=ta[:, cs], in1=tb[:, cs], op=ALU.mult)
+
+        def tail(r, half, ta):
+            tcl = ep2.tile([P, HALF], F32, name="tcl")
+            nc.vector.tensor_scalar(out=tcl[:], in0=ta[:], scalar1=-CUT, scalar2=CUT, op0=ALU.max, op1=ALU.min)
+            nc.vector.tensor_scalar_min(out=ta[:], in0=ta[:], scalar1=85.0)
+            nc.scalar.activation(out=tcl[:], in_=tcl[:], func=ACT.Tanh, scale=1.0 / RT2)
+            tsq = ep2.tile([P, HALF], F32, name="tsq")
+            nc.scalar.activation(out=tsq[:], in_=ta[:], func=ACT.Square)
+            nc.vector.tensor_scalar_max(out=tsq[:], in0=tsq[:], scalar1=CUT * CUT)
+            te = ep2.tile([P, HALF], F32, name="te")
+            nc.vector.scalar_tensor_tensor(out=te[:], in0=tsq[:], scalar=1.0, in1=tsq[:], op0=ALU.add, op1=ALU.mult)
+            nc.scalar.activation(out=te[:], in_=te[:], func=ACT.Sqrt, scale=4.0)
+            nc.vector.scalar_tensor_tensor(out=te[:], in0=tsq[:], scalar=2.0, in1=te[:], op0=ALU.mult, op1=ALU.add)
+            nc.scalar.activation(out=te[:], in_=te[:], func=ACT.Ln, bias=1.0)
+            nc.vector.scalar_tensor_tensor(out=te[:], in0=te[:], scalar=c_out[:], in1=tcl[:], op0=ALU.mult, op1=ALU.mult)
+            nc.sync.dma_start(
+                out=out[r].rearrange("k h w -> k (h w)")[:, half * HALF : (half + 1) * HALF], in_=te[:]
+            )
+
+        fgh = norms(0)
+        for r in range(BATCH):
+            nxt = norms(r + 1) if r + 1 < BATCH else None
+            for half in range(2):
+                ta = ep1.tile([P, HALF], F32, name="ta")
+                tb = ep1.tile([P, HALF], F32, name="tb")
+                for i in range(4 * half, 4 * half + 4):
+                    sub_tile(r, i, fgh, ta, tb)
+                tail(r, half, ta)
+            if r + 3 < BATCH:
+                load_z(r + 3)
+            fgh = nxt

@@ -20,6 +20,7 @@ BATCH = 4
 PIX = 4096
 SUB = 512
 HALF = 2048
+QUART = 1024
 BLK = 128
 EPS = 1e-5
 CUT = 0.005
@@ -32,7 +33,7 @@ def tile_hyperboliclayer_t_kernel(tc, z, p, normals, out):
     nc = tc.nc
     with ExitStack() as ctx:
         const = ctx.enter_context(tc.tile_pool(name="const", bufs=1))
-        zpool = ctx.enter_context(tc.tile_pool(name="zpool", bufs=3))
+        zpool = ctx.enter_context(tc.tile_pool(name="zpool", bufs=2))
         ypool = ctx.enter_context(tc.tile_pool(name="ypool", bufs=3))
         small = ctx.enter_context(tc.tile_pool(name="small", bufs=2))
         ep1 = ctx.enter_context(tc.tile_pool(name="ep1", bufs=2))
@@ -58,7 +59,7 @@ def tile_hyperboliclayer_t_kernel(tc, z, p, normals, out):
             nc.sync.dma_start(out=z_sb[:], in_=z[r].rearrange("(q t) h w -> q t (h w)", t=PACK))
             z_tiles.append(z_sb)
 
-        for r in range(3):
+        for r in range(2):
             load_z(r)
 
         junk_c = const.tile([P, 512], F32)
@@ -70,8 +71,8 @@ def tile_hyperboliclayer_t_kernel(tc, z, p, normals, out):
         nc.vector.tensor_tensor(out=prod[:], in0=p_sb[:], in1=n_sb[:], op=ALU.mult)
         spn = const.tile([P, 1], F32)
         nc.vector.reduce_sum(out=spn[:], in_=prod[:], axis=AX.X)
-        c_4pw = const.tile([P, 1], F32)
-        nc.vector.tensor_scalar(out=c_4pw[:], in0=spn[:], scalar1=-4.0, scalar2=None, op0=ALU.mult)
+        c_2pw = const.tile([P, 1], F32)
+        nc.vector.tensor_scalar(out=c_2pw[:], in0=spn[:], scalar1=-2.0, scalar2=None, op0=ALU.mult)
         c_m2pw = const.tile([P, 1], F32)
         nc.vector.tensor_scalar(out=c_m2pw[:], in0=spn[:], scalar1=2.0, scalar2=None, op0=ALU.mult)
         c_2b = const.tile([P, 1], F32)
@@ -82,6 +83,8 @@ def tile_hyperboliclayer_t_kernel(tc, z, p, normals, out):
         nc.vector.tensor_scalar(out=c_mpp[:], in0=pp[:], scalar1=-1.0, scalar2=None, op0=ALU.mult)
         c_b = const.tile([P, 1], F32)
         nc.vector.tensor_scalar(out=c_b[:], in0=pp[:], scalar1=-1.0, scalar2=1.0, op0=ALU.mult, op1=ALU.add)
+        c_2pwb = const.tile([P, 1], F32)
+        nc.vector.tensor_tensor(out=c_2pwb[:], in0=c_2pw[:], in1=c_b[:], op=ALU.mult)
         c_1 = const.tile([P, 1], F32)
         nc.vector.tensor_tensor(out=c_1[:], in0=c_b[:], in1=ww[:], op=ALU.mult)
         c_i1 = const.tile([P, 1], F32)
@@ -123,15 +126,21 @@ def tile_hyperboliclayer_t_kernel(tc, z, p, normals, out):
                         out=junk[:], in_=zt[:, u, :, :].rearrange("p t q -> p (t q)"), func=ACT.Square,
                         accum_out=s[:, blk : blk + 1],
                     )
+            nc.vector.tensor_scalar_max(out=s[:], in0=s[:], scalar1=1e-30)
+            r0 = small.tile([P, nblk], F32, name="r0")
+            nc.scalar.activation(out=r0[:], in_=s[:], func=ACT.Abs_reciprocal_sqrt)
+            nw = small.tile([P, nblk], F32, name="nw")
+            nc.vector.tensor_tensor(out=nw[:], in0=r0[:], in1=r0[:], op=ALU.mult)
+            nc.vector.tensor_tensor(out=nw[:], in0=nw[:], in1=s[:], op=ALU.mult)
+            nc.vector.tensor_scalar(out=nw[:], in0=nw[:], scalar1=-0.5, scalar2=1.5, op0=ALU.mult, op1=ALU.add)
+            rn = small.tile([P, nblk], F32, name="rn")
+            nc.vector.tensor_tensor(out=rn[:], in0=r0[:], in1=nw[:], op=ALU.mult)
             n = small.tile([P, nblk], F32, name="n")
-            nc.scalar.activation(out=n[:], in_=s[:], func=ACT.Sqrt)
-            nc.vector.tensor_scalar_max(out=n[:], in0=n[:], scalar1=1e-15)
+            nc.vector.tensor_tensor(out=n[:], in0=s[:], in1=rn[:], op=ALU.mult)
             th = small.tile([P, nblk], F32, name="th")
             nc.scalar.activation(out=th[:], in_=n[:], func=ACT.Tanh)
             e = small.tile([P, nblk], F32, name="e")
             nc.scalar.activation(out=e[:], in_=n[:], func=ACT.Exp, scale=-2.0)
-            rn = small.tile([P, nblk], F32, name="rn")
-            nc.vector.reciprocal(out=rn[:], in_=n[:])
             f = small.tile([P, nblk], F32, name="f")
             nc.vector.tensor_tensor(out=f[:], in0=th[:], in1=rn[:], op=ALU.mult)
             d = small.tile([P, nblk], F32, name="d")
@@ -152,15 +161,15 @@ def tile_hyperboliclayer_t_kernel(tc, z, p, normals, out):
                     dst[:, j * BLK : (j + 1) * BLK], col_tile[:, b : b + 1].to_broadcast([P, P]), ident_f[:]
                 )
 
-        def sub_tile(r, i, fgh, ta, tb):
+        def front(r, i, fgh, ta, tb):
             f, g, h = fgh
             z_sb = z_tiles[r]
-            cs = slice((i % 4) * SUB, (i % 4 + 1) * SUB)
+            cs = slice(i * SUB, (i + 1) * SUB)
             fb = ps_fb.tile([P, SUB], F32, name="fb")
             spread(fb, f, 4 * i)
             yg = ypool.tile([P, SUB, PACK], BF16, align_bytes=64, name="yg")
             nc.vector.tensor_tensor(
-                out=yg[:], in0=z_sb[:, :, i * SUB : (i + 1) * SUB].rearrange("p t w -> p w t"),
+                out=yg[:], in0=z_sb[:, :, cs].rearrange("p t w -> p w t"),
                 in1=fb[:].unsqueeze(2).to_broadcast([P, SUB, PACK]), op=ALU.mult,
             )
             codes = ypool.tile([P, SUB], U32, align_bytes=64, name="codes")
@@ -180,49 +189,62 @@ def tile_hyperboliclayer_t_kernel(tc, z, p, normals, out):
             )
             gb = ps_ep.tile([P, SUB], F32, name="gb")
             spread(gb, g, 4 * i)
-            hb = ps_ep.tile([P, SUB], F32, name="hb")
-            spread(hb, h, 4 * i)
-            nc.scalar.activation(out=ta[:, cs], in_=a_ps[:], func=ACT.Identity, scale=c_4pw[:], bias=c_4pw[:])
-            nc.scalar.activation(out=tb[:, cs], in_=a_ps[:], func=ACT.Identity, scale=2.0, bias=c_1pp[:])
+            nc.scalar.activation(out=ta[:, cs], in_=a_ps[:], func=ACT.Identity, scale=2.0, bias=c_1pp[:])
+            nc.vector.scalar_tensor_tensor(
+                out=tb[:, cs], in0=gb[:], scalar=c_mpp[:], in1=ta[:, cs], op0=ALU.mult, op1=ALU.add)
+            nc.gpsimd.tensor_scalar(
+                out=ta[:, cs], in0=ta[:, cs], scalar1=c_2pw[:], scalar2=c_2pwb[:], op0=ALU.mult, op1=ALU.add)
             nc.vector.scalar_tensor_tensor(
                 out=ta[:, cs], in0=gb[:], scalar=c_m2pw[:], in1=ta[:, cs], op0=ALU.mult, op1=ALU.add)
             nc.vector.scalar_tensor_tensor(
                 out=ta[:, cs], in0=w_ps[:], scalar=c_2b[:], in1=ta[:, cs], op0=ALU.mult, op1=ALU.add)
-            nc.vector.scalar_tensor_tensor(
-                out=tb[:, cs], in0=gb[:], scalar=c_mpp[:], in1=tb[:, cs], op0=ALU.mult, op1=ALU.add)
-            nc.scalar.activation(out=tb[:, cs], in_=tb[:, cs], func=ACT.Abs_reciprocal_sqrt, scale=EPS)
-            nc.scalar.activation(out=tb[:, cs], in_=tb[:, cs], func=ACT.Square)
-            nc.vector.scalar_tensor_tensor(
-                out=tb[:, cs], in0=hb[:], scalar=c_i1[:], in1=tb[:, cs], op0=ALU.mult, op1=ALU.min)
-            nc.vector.tensor_tensor(out=ta[:, cs], in0=ta[:, cs], in1=tb[:, cs], op=ALU.mult)
 
-        def tail(r, half, ta):
-            tcl = ep2.tile([P, HALF], F32, name="tcl")
-            nc.vector.tensor_scalar(out=tcl[:], in0=ta[:], scalar1=-CUT, scalar2=CUT, op0=ALU.max, op1=ALU.min)
-            nc.vector.tensor_scalar_min(out=ta[:], in0=ta[:], scalar1=85.0)
-            nc.scalar.activation(out=tcl[:], in_=tcl[:], func=ACT.Tanh, scale=1.0 / RT2)
-            tsq = ep2.tile([P, HALF], F32, name="tsq")
-            nc.scalar.activation(out=tsq[:], in_=ta[:], func=ACT.Square)
-            nc.vector.tensor_scalar_max(out=tsq[:], in0=tsq[:], scalar1=CUT * CUT)
-            te = ep2.tile([P, HALF], F32, name="te")
-            nc.vector.scalar_tensor_tensor(out=te[:], in0=tsq[:], scalar=1.0, in1=tsq[:], op0=ALU.add, op1=ALU.mult)
-            nc.scalar.activation(out=te[:], in_=te[:], func=ACT.Sqrt, scale=4.0)
-            nc.vector.scalar_tensor_tensor(out=te[:], in0=tsq[:], scalar=2.0, in1=te[:], op0=ALU.mult, op1=ALU.add)
-            nc.scalar.activation(out=te[:], in_=te[:], func=ACT.Ln, bias=1.0)
-            nc.vector.scalar_tensor_tensor(out=te[:], in0=te[:], scalar=c_out[:], in1=tcl[:], op0=ALU.mult, op1=ALU.mult)
-            nc.sync.dma_start(
-                out=out[r].rearrange("k h w -> k (h w)")[:, half * HALF : (half + 1) * HALF], in_=te[:]
-            )
+        def back(r, fgh, ta, tb):
+            h = fgh[2]
+            nc.scalar.activation(out=tb[:], in_=tb[:], func=ACT.Abs_reciprocal_sqrt, scale=EPS)
+            for qt in range(PIX // QUART):
+                qs = slice(qt * QUART, (qt + 1) * QUART)
+                nc.gpsimd.tensor_tensor(out=tb[:, qs], in0=tb[:, qs], in1=tb[:, qs], op=ALU.mult)
+                for i in range(2 * qt, 2 * qt + 2):
+                    cs = slice(i * SUB, (i + 1) * SUB)
+                    hb = ps_ep.tile([P, SUB], F32, name="hb")
+                    spread(hb, h, 4 * i)
+                    nc.vector.scalar_tensor_tensor(
+                        out=tb[:, cs], in0=hb[:], scalar=c_i1[:], in1=tb[:, cs], op0=ALU.mult, op1=ALU.min)
+                nc.gpsimd.tensor_tensor(out=ta[:, qs], in0=ta[:, qs], in1=tb[:, qs], op=ALU.mult)
+                nc.gpsimd.tensor_scalar(
+                    out=tb[:, qs], in0=ta[:, qs], scalar1=-CUT, scalar2=CUT, op0=ALU.max, op1=ALU.min)
+                nc.gpsimd.tensor_scalar(
+                    out=ta[:, qs], in0=ta[:, qs], scalar1=85.0, scalar2=0.0, op0=ALU.min, op1=ALU.add)
+            tsq = ep2.tile([P, PIX], F32, name="tsq")
+            for half in range(2):
+                hs = slice(half * HALF, (half + 1) * HALF)
+                nc.scalar.activation(out=tsq[:, hs], in_=ta[:, hs], func=ACT.Square)
+                nc.gpsimd.tensor_scalar(
+                    out=tsq[:, hs], in0=tsq[:, hs], scalar1=CUT * CUT, scalar2=0.0, op0=ALU.max, op1=ALU.add)
+                nc.vector.scalar_tensor_tensor(
+                    out=ta[:, hs], in0=tsq[:, hs], scalar=1.0, in1=tsq[:, hs], op0=ALU.add, op1=ALU.mult)
+            nc.scalar.activation(out=tb[:], in_=tb[:], func=ACT.Tanh, scale=1.0 / RT2)
+            nc.scalar.activation(out=ta[:], in_=ta[:], func=ACT.Sqrt, scale=4.0)
+            for half in range(2):
+                hs = slice(half * HALF, (half + 1) * HALF)
+                nc.vector.scalar_tensor_tensor(
+                    out=ta[:, hs], in0=tsq[:, hs], scalar=2.0, in1=ta[:, hs], op0=ALU.mult, op1=ALU.add)
+            nc.scalar.activation(out=ta[:], in_=ta[:], func=ACT.Ln, bias=1.0)
+            for half in range(2):
+                hs = slice(half * HALF, (half + 1) * HALF)
+                nc.vector.scalar_tensor_tensor(
+                    out=ta[:, hs], in0=ta[:, hs], scalar=c_out[:], in1=tb[:, hs], op0=ALU.mult, op1=ALU.mult)
+                nc.sync.dma_start(out=out[r].rearrange("k h w -> k (h w)")[:, hs], in_=ta[:, hs])
 
         fgh = norms(0)
         for r in range(BATCH):
             nxt = norms(r + 1) if r + 1 < BATCH else None
-            for half in range(2):
-                ta = ep1.tile([P, HALF], F32, name="ta")
-                tb = ep1.tile([P, HALF], F32, name="tb")
-                for i in range(4 * half, 4 * half + 4):
-                    sub_tile(r, i, fgh, ta, tb)
-                tail(r, half, ta)
-            if r + 3 < BATCH:
-                load_z(r + 3)
+            ta = ep1.tile([P, PIX], F32, name="ta")
+            tb = ep1.tile([P, PIX], F32, name="tb")
+            for i in range(PIX // SUB):
+                front(r, i, fgh, ta, tb)
+            if r + 2 < BATCH:
+                load_z(r + 2)
+            back(r, fgh, ta, tb)
             fgh = nxt

@@ -21,6 +21,8 @@ PIX = 4096
 SUB = 512
 HALF = 2048
 QUART = 1024
+FIRST_BATCHES = (0, 8, 16, 32)
+LAST_CUTS = (0, 2048, 3072, 4096)
 BLK = 128
 EPS = 1e-5
 CUT = 0.005
@@ -54,13 +56,16 @@ def tile_hyperboliclayer_t_kernel(tc, z, p, normals, out):
 
         z_tiles = []
 
-        def load_z(r):
+        def load_z(r, pieces):
             z_sb = zpool.tile([P, PACK, PIX], BF16, name="z_sb")
-            nc.sync.dma_start(out=z_sb[:], in_=z[r].rearrange("(q t) h w -> q t (h w)", t=PACK))
+            src = z[r].rearrange("(q t) h w -> q t (h w)", t=PACK)
+            step = PIX // pieces
+            for c in range(pieces):
+                nc.sync.dma_start(out=z_sb[:, :, c * step : (c + 1) * step], in_=src[:, :, c * step : (c + 1) * step])
             z_tiles.append(z_sb)
 
-        for r in range(2):
-            load_z(r)
+        load_z(0, 4)
+        load_z(1, 1)
 
         junk_c = const.tile([P, 512], F32)
         pp = const.tile([P, 1], F32)
@@ -109,50 +114,47 @@ def tile_hyperboliclayer_t_kernel(tc, z, p, normals, out):
             out=wcodes[:].bitcast(FP8X4), scales=wscale[:], in_=wgrp[:].rearrange("q o c t -> q (o c t)")
         )
 
-        def norms(r):
+        NBLK = PIX // BLK
+
+        NAMES = ("s", "r0", "nw", "rn", "n", "th", "e", "f", "d", "rd", "g", "h")
+        per_pixel = {}
+
+        def norm_tiles(r):
+            per_pixel[r] = dict((nm, small.tile([P, NBLK], F32, name=nm)) for nm in NAMES)
+
+        def norm_blocks(r, c0, c1):
             z_sb = z_tiles[r]
-            nblk = PIX // BLK
-            s = small.tile([P, nblk], F32, name="s")
-            for b2 in range(nblk // 2):
+            for b2 in range(c0 // 2, c1 // 2):
                 zt = ps_zt.tile([P, 2, PACK, P], BF16, tag="zt", name="zt")
                 for u in range(2):
                     blk = 2 * b2 + u
-                    for t in range(PACK):
-                        nc.tensor.transpose(zt[:, u, t, :], z_sb[:, t, blk * BLK : (blk + 1) * BLK], ident_bf[:])
+                    for k in range(PACK):
+                        nc.tensor.transpose(zt[:, u, k, :], z_sb[:, k, blk * BLK : (blk + 1) * BLK], ident_bf[:])
                 for u in range(2):
                     blk = 2 * b2 + u
                     junk = small.tile([P, PACK * P], BF16, name="junk")
                     nc.scalar.activation(
                         out=junk[:], in_=zt[:, u, :, :].rearrange("p t q -> p (t q)"), func=ACT.Square,
-                        accum_out=s[:, blk : blk + 1],
+                        accum_out=per_pixel[r]["s"][:, blk : blk + 1],
                     )
-            nc.vector.tensor_scalar_max(out=s[:], in0=s[:], scalar1=1e-30)
-            r0 = small.tile([P, nblk], F32, name="r0")
-            nc.scalar.activation(out=r0[:], in_=s[:], func=ACT.Abs_reciprocal_sqrt)
-            nw = small.tile([P, nblk], F32, name="nw")
-            nc.vector.tensor_tensor(out=nw[:], in0=r0[:], in1=r0[:], op=ALU.mult)
-            nc.vector.tensor_tensor(out=nw[:], in0=nw[:], in1=s[:], op=ALU.mult)
-            nc.vector.tensor_scalar(out=nw[:], in0=nw[:], scalar1=-0.5, scalar2=1.5, op0=ALU.mult, op1=ALU.add)
-            rn = small.tile([P, nblk], F32, name="rn")
-            nc.vector.tensor_tensor(out=rn[:], in0=r0[:], in1=nw[:], op=ALU.mult)
-            n = small.tile([P, nblk], F32, name="n")
-            nc.vector.tensor_tensor(out=n[:], in0=s[:], in1=rn[:], op=ALU.mult)
-            th = small.tile([P, nblk], F32, name="th")
-            nc.scalar.activation(out=th[:], in_=n[:], func=ACT.Tanh)
-            e = small.tile([P, nblk], F32, name="e")
-            nc.scalar.activation(out=e[:], in_=n[:], func=ACT.Exp, scale=-2.0)
-            f = small.tile([P, nblk], F32, name="f")
-            nc.vector.tensor_tensor(out=f[:], in0=th[:], in1=rn[:], op=ALU.mult)
-            d = small.tile([P, nblk], F32, name="d")
-            nc.vector.tensor_scalar(out=d[:], in0=e[:], scalar1=1.0, scalar2=None, op0=ALU.add)
-            rd = small.tile([P, nblk], F32, name="rd")
-            nc.vector.reciprocal(out=rd[:], in_=d[:])
-            g = small.tile([P, nblk], F32, name="g")
-            nc.vector.scalar_tensor_tensor(out=g[:], in0=e[:], scalar=4.0, in1=rd[:], op0=ALU.mult, op1=ALU.mult)
-            nc.vector.tensor_tensor(out=g[:], in0=g[:], in1=rd[:], op=ALU.mult)
-            h = small.tile([P, nblk], F32, name="h")
-            nc.vector.reciprocal(out=h[:], in_=g[:])
-            return f, g, h
+
+        def norm_chain(r, c0, c1):
+            v = dict((nm, per_pixel[r][nm][:, c0:c1]) for nm in NAMES)
+            nc.vector.tensor_scalar_max(out=v["s"], in0=v["s"], scalar1=1e-30)
+            nc.scalar.activation(out=v["r0"], in_=v["s"], func=ACT.Abs_reciprocal_sqrt)
+            nc.vector.tensor_tensor(out=v["nw"], in0=v["r0"], in1=v["r0"], op=ALU.mult)
+            nc.vector.tensor_tensor(out=v["nw"], in0=v["nw"], in1=v["s"], op=ALU.mult)
+            nc.vector.tensor_scalar(out=v["nw"], in0=v["nw"], scalar1=-0.5, scalar2=1.5, op0=ALU.mult, op1=ALU.add)
+            nc.vector.tensor_tensor(out=v["rn"], in0=v["r0"], in1=v["nw"], op=ALU.mult)
+            nc.vector.tensor_tensor(out=v["n"], in0=v["s"], in1=v["rn"], op=ALU.mult)
+            nc.scalar.activation(out=v["th"], in_=v["n"], func=ACT.Tanh)
+            nc.scalar.activation(out=v["e"], in_=v["n"], func=ACT.Exp, scale=-2.0)
+            nc.vector.tensor_tensor(out=v["f"], in0=v["th"], in1=v["rn"], op=ALU.mult)
+            nc.vector.tensor_scalar(out=v["d"], in0=v["e"], scalar1=1.0, scalar2=None, op0=ALU.add)
+            nc.vector.reciprocal(out=v["rd"], in_=v["d"])
+            nc.vector.scalar_tensor_tensor(out=v["g"], in0=v["e"], scalar=4.0, in1=v["rd"], op0=ALU.mult, op1=ALU.mult)
+            nc.vector.tensor_tensor(out=v["g"], in0=v["g"], in1=v["rd"], op=ALU.mult)
+            nc.vector.reciprocal(out=v["h"], in_=v["g"])
 
         def spread(dst, col_tile, first_blk):
             for j in range(SUB // BLK):
@@ -161,8 +163,8 @@ def tile_hyperboliclayer_t_kernel(tc, z, p, normals, out):
                     dst[:, j * BLK : (j + 1) * BLK], col_tile[:, b : b + 1].to_broadcast([P, P]), ident_f[:]
                 )
 
-        def front(r, i, fgh, ta, tb):
-            f, g, h = fgh
+        def front(r, i, ta, tb):
+            f, g = per_pixel[r]["f"], per_pixel[r]["g"]
             z_sb = z_tiles[r]
             cs = slice(i * SUB, (i + 1) * SUB)
             fb = ps_fb.tile([P, SUB], F32, name="fb")
@@ -192,59 +194,67 @@ def tile_hyperboliclayer_t_kernel(tc, z, p, normals, out):
             nc.scalar.activation(out=ta[:, cs], in_=a_ps[:], func=ACT.Identity, scale=2.0, bias=c_1pp[:])
             nc.vector.scalar_tensor_tensor(
                 out=tb[:, cs], in0=gb[:], scalar=c_mpp[:], in1=ta[:, cs], op0=ALU.mult, op1=ALU.add)
-            nc.gpsimd.tensor_scalar(
+            nc.vector.tensor_scalar(
                 out=ta[:, cs], in0=ta[:, cs], scalar1=c_2pw[:], scalar2=c_2pwb[:], op0=ALU.mult, op1=ALU.add)
             nc.vector.scalar_tensor_tensor(
                 out=ta[:, cs], in0=gb[:], scalar=c_m2pw[:], in1=ta[:, cs], op0=ALU.mult, op1=ALU.add)
             nc.vector.scalar_tensor_tensor(
                 out=ta[:, cs], in0=w_ps[:], scalar=c_2b[:], in1=ta[:, cs], op0=ALU.mult, op1=ALU.add)
 
-        def back(r, fgh, ta, tb):
-            h = fgh[2]
-            nc.scalar.activation(out=tb[:], in_=tb[:], func=ACT.Abs_reciprocal_sqrt, scale=EPS)
-            for qt in range(PIX // QUART):
-                qs = slice(qt * QUART, (qt + 1) * QUART)
-                nc.gpsimd.tensor_tensor(out=tb[:, qs], in0=tb[:, qs], in1=tb[:, qs], op=ALU.mult)
-                for i in range(2 * qt, 2 * qt + 2):
+        def back(r, ta, tb, tsq, lo, hi):
+            h = per_pixel[r]["h"]
+            al = slice(lo, hi)
+            piece = min(HALF, hi - lo)
+            parts = [slice(c0, c0 + piece) for c0 in range(lo, hi, piece)]
+            nc.scalar.activation(out=tb[:, al], in_=tb[:, al], func=ACT.Abs_reciprocal_sqrt, scale=EPS)
+            nc.scalar.activation(out=tb[:, al], in_=tb[:, al], func=ACT.Square)
+            for q0 in range(lo, hi, QUART):
+                qs = slice(q0, q0 + QUART)
+                for i in range(q0 // SUB, q0 // SUB + QUART // SUB):
                     cs = slice(i * SUB, (i + 1) * SUB)
                     hb = ps_ep.tile([P, SUB], F32, name="hb")
                     spread(hb, h, 4 * i)
                     nc.vector.scalar_tensor_tensor(
                         out=tb[:, cs], in0=hb[:], scalar=c_i1[:], in1=tb[:, cs], op0=ALU.mult, op1=ALU.min)
-                nc.gpsimd.tensor_tensor(out=ta[:, qs], in0=ta[:, qs], in1=tb[:, qs], op=ALU.mult)
-                nc.gpsimd.tensor_scalar(
+                nc.vector.tensor_tensor(out=ta[:, qs], in0=ta[:, qs], in1=tb[:, qs], op=ALU.mult)
+                nc.vector.tensor_scalar(
                     out=tb[:, qs], in0=ta[:, qs], scalar1=-CUT, scalar2=CUT, op0=ALU.max, op1=ALU.min)
-                nc.gpsimd.tensor_scalar(
-                    out=ta[:, qs], in0=ta[:, qs], scalar1=85.0, scalar2=0.0, op0=ALU.min, op1=ALU.add)
-            tsq = ep2.tile([P, PIX], F32, name="tsq")
-            for half in range(2):
-                hs = slice(half * HALF, (half + 1) * HALF)
+                nc.vector.tensor_scalar_min(out=ta[:, qs], in0=ta[:, qs], scalar1=85.0)
+            for hs in parts:
                 nc.scalar.activation(out=tsq[:, hs], in_=ta[:, hs], func=ACT.Square)
-                nc.gpsimd.tensor_scalar(
-                    out=tsq[:, hs], in0=tsq[:, hs], scalar1=CUT * CUT, scalar2=0.0, op0=ALU.max, op1=ALU.add)
+                nc.vector.tensor_scalar_max(out=tsq[:, hs], in0=tsq[:, hs], scalar1=CUT * CUT)
                 nc.vector.scalar_tensor_tensor(
                     out=ta[:, hs], in0=tsq[:, hs], scalar=1.0, in1=tsq[:, hs], op0=ALU.add, op1=ALU.mult)
-            nc.scalar.activation(out=tb[:], in_=tb[:], func=ACT.Tanh, scale=1.0 / RT2)
-            nc.scalar.activation(out=ta[:], in_=ta[:], func=ACT.Sqrt, scale=4.0)
-            for half in range(2):
-                hs = slice(half * HALF, (half + 1) * HALF)
+            nc.scalar.activation(out=tb[:, al], in_=tb[:, al], func=ACT.Tanh, scale=1.0 / RT2)
+            nc.scalar.activation(out=ta[:, al], in_=ta[:, al], func=ACT.Sqrt, scale=4.0)
+            for hs in parts:
                 nc.vector.scalar_tensor_tensor(
                     out=ta[:, hs], in0=tsq[:, hs], scalar=2.0, in1=ta[:, hs], op0=ALU.mult, op1=ALU.add)
-            nc.scalar.activation(out=ta[:], in_=ta[:], func=ACT.Ln, bias=1.0)
-            for half in range(2):
-                hs = slice(half * HALF, (half + 1) * HALF)
+            nc.scalar.activation(out=ta[:, al], in_=ta[:, al], func=ACT.Ln, bias=1.0)
+            for hs in parts:
                 nc.vector.scalar_tensor_tensor(
                     out=ta[:, hs], in0=ta[:, hs], scalar=c_out[:], in1=tb[:, hs], op0=ALU.mult, op1=ALU.mult)
                 nc.sync.dma_start(out=out[r].rearrange("k h w -> k (h w)")[:, hs], in_=ta[:, hs])
 
-        fgh = norms(0)
+        norm_tiles(0)
+        for c0, c1 in zip(FIRST_BATCHES[:-1], FIRST_BATCHES[1:]):
+            norm_blocks(0, c0, c1)
+            norm_chain(0, c0, c1)
         for r in range(BATCH):
-            nxt = norms(r + 1) if r + 1 < BATCH else None
+            more = r + 1 < BATCH
+            if more:
+                norm_tiles(r + 1)
             ta = ep1.tile([P, PIX], F32, name="ta")
             tb = ep1.tile([P, PIX], F32, name="tb")
-            for i in range(PIX // SUB):
-                front(r, i, fgh, ta, tb)
-            if r + 2 < BATCH:
-                load_z(r + 2)
-            back(r, fgh, ta, tb)
-            fgh = nxt
+            tsq = ep2.tile([P, PIX], F32, name="tsq")
+            cuts = (0, PIX) if more else LAST_CUTS
+            for lo, hi in zip(cuts[:-1], cuts[1:]):
+                for i in range(lo // SUB, hi // SUB):
+                    front(r, i, ta, tb)
+                    if more:
+                        norm_blocks(r + 1, 4 * i, 4 * i + 4)
+                if more:
+                    norm_chain(r + 1, 0, NBLK)
+                if r + 2 < BATCH:
+                    load_z(r + 2, 1)
+                back(r, ta, tb, tsq, lo, hi)

@@ -163,22 +163,31 @@ def tile_hyperboliclayer_t_kernel(tc, z, p, normals, out):
                     dst[:, j * BLK : (j + 1) * BLK], col_tile[:, b : b + 1].to_broadcast([P, P]), ident_f[:]
                 )
 
-        def front(r, i, ta, tb):
-            f, g = per_pixel[r]["f"], per_pixel[r]["g"]
-            z_sb = z_tiles[r]
+        ygs = {}
+        banks = {}
+
+        def front_y(r, i):
             cs = slice(i * SUB, (i + 1) * SUB)
             fb = ps_fb.tile([P, SUB], F32, name="fb")
-            spread(fb, f, 4 * i)
+            spread(fb, per_pixel[r]["f"], 4 * i)
             yg = ypool.tile([P, SUB, PACK], BF16, align_bytes=64, name="yg")
             nc.vector.tensor_tensor(
-                out=yg[:], in0=z_sb[:, :, cs].rearrange("p t w -> p w t"),
+                out=yg[:], in0=z_tiles[r][:, :, cs].rearrange("p t w -> p w t"),
                 in1=fb[:].unsqueeze(2).to_broadcast([P, SUB, PACK]), op=ALU.mult,
             )
+            ygs[(r, i)] = yg
+
+        def front_q(r, i):
             codes = ypool.tile([P, SUB], U32, align_bytes=64, name="codes")
             scale = ypool.tile([P, SUB], U8, align_bytes=64, name="scale")
             nc.vector.quantize_mx(
-                out=codes[:].bitcast(FP8X4), scales=scale[:], in_=yg[:].rearrange("p w t -> p (w t)")
+                out=codes[:].bitcast(FP8X4), scales=scale[:], in_=ygs[(r, i)][:].rearrange("p w t -> p (w t)")
             )
+            banks[(r, i)] = (codes, scale)
+
+        def front_mx(r, i, ta):
+            cs = slice(i * SUB, (i + 1) * SUB)
+            codes, scale = banks[(r, i)]
             a_ps = ps_ep.tile([P, SUB], F32, name="a_ps")
             nc.tensor.matmul_mx(
                 out=a_ps[:], lhsT=wcodes[:, 0:P].bitcast(FP8X4), lhsT_scale=wscale[:, 0:P],
@@ -190,16 +199,27 @@ def tile_hyperboliclayer_t_kernel(tc, z, p, normals, out):
                 rhs=codes[:].bitcast(FP8X4), rhs_scale=scale[:], start=True, stop=True,
             )
             gb = ps_ep.tile([P, SUB], F32, name="gb")
-            spread(gb, g, 4 * i)
+            spread(gb, per_pixel[r]["g"], 4 * i)
             nc.scalar.activation(out=ta[:, cs], in_=a_ps[:], func=ACT.Identity, scale=2.0, bias=c_1pp[:])
+            banks[(r, i)] = (w_ps, gb)
+
+        def front_e1(r, i, ta, tb):
+            cs = slice(i * SUB, (i + 1) * SUB)
+            gb = banks[(r, i)][1]
             nc.vector.scalar_tensor_tensor(
                 out=tb[:, cs], in0=gb[:], scalar=c_mpp[:], in1=ta[:, cs], op0=ALU.mult, op1=ALU.add)
             nc.vector.tensor_scalar(
                 out=ta[:, cs], in0=ta[:, cs], scalar1=c_2pw[:], scalar2=c_2pwb[:], op0=ALU.mult, op1=ALU.add)
+
+        def front_e2(r, i, ta):
+            cs = slice(i * SUB, (i + 1) * SUB)
             nc.vector.scalar_tensor_tensor(
-                out=ta[:, cs], in0=gb[:], scalar=c_m2pw[:], in1=ta[:, cs], op0=ALU.mult, op1=ALU.add)
+                out=ta[:, cs], in0=banks[(r, i)][1][:], scalar=c_m2pw[:], in1=ta[:, cs], op0=ALU.mult, op1=ALU.add)
+
+        def front_e3(r, i, ta):
+            cs = slice(i * SUB, (i + 1) * SUB)
             nc.vector.scalar_tensor_tensor(
-                out=ta[:, cs], in0=w_ps[:], scalar=c_2b[:], in1=ta[:, cs], op0=ALU.mult, op1=ALU.add)
+                out=ta[:, cs], in0=banks[(r, i)][0][:], scalar=c_2b[:], in1=ta[:, cs], op0=ALU.mult, op1=ALU.add)
 
         def back(r, ta, tb, tsq, lo, hi):
             h = per_pixel[r]["h"]
@@ -208,21 +228,35 @@ def tile_hyperboliclayer_t_kernel(tc, z, p, normals, out):
             parts = [slice(c0, c0 + piece) for c0 in range(lo, hi, piece)]
             nc.scalar.activation(out=tb[:, al], in_=tb[:, al], func=ACT.Abs_reciprocal_sqrt, scale=EPS)
             nc.scalar.activation(out=tb[:, al], in_=tb[:, al], func=ACT.Square)
-            for q0 in range(lo, hi, QUART):
-                qs = slice(q0, q0 + QUART)
-                for i in range(q0 // SUB, q0 // SUB + QUART // SUB):
-                    cs = slice(i * SUB, (i + 1) * SUB)
-                    hb = ps_ep.tile([P, SUB], F32, name="hb")
-                    spread(hb, h, 4 * i)
-                    nc.vector.scalar_tensor_tensor(
-                        out=tb[:, cs], in0=hb[:], scalar=c_i1[:], in1=tb[:, cs], op0=ALU.mult, op1=ALU.min)
-                nc.vector.tensor_tensor(out=ta[:, qs], in0=ta[:, qs], in1=tb[:, qs], op=ALU.mult)
+            def limit(i):
+                cs = slice(i * SUB, (i + 1) * SUB)
+                hb = ps_ep.tile([P, SUB], F32, name="hb")
+                spread(hb, h, 4 * i)
+                nc.vector.scalar_tensor_tensor(
+                    out=tb[:, cs], in0=hb[:], scalar=c_i1[:], in1=tb[:, cs], op0=ALU.mult, op1=ALU.min)
+
+            def clamp(qs):
                 nc.vector.tensor_scalar(
                     out=tb[:, qs], in0=ta[:, qs], scalar1=-CUT, scalar2=CUT, op0=ALU.max, op1=ALU.min)
                 nc.vector.tensor_scalar_min(out=ta[:, qs], in0=ta[:, qs], scalar1=85.0)
+
+            quarts = [slice(q0, q0 + QUART) for q0 in range(lo, hi, QUART)]
+            first = lo // SUB
+            limit(first)
+            limit(first + 1)
+            for n, qs in enumerate(quarts):
+                if n + 1 < len(quarts):
+                    limit(first + 2 * n + 2)
+                    limit(first + 2 * n + 3)
+                nc.vector.tensor_tensor(out=ta[:, qs], in0=ta[:, qs], in1=tb[:, qs], op=ALU.mult)
+                if n > 0:
+                    clamp(quarts[n - 1])
+            clamp(quarts[-1])
             for hs in parts:
                 nc.scalar.activation(out=tsq[:, hs], in_=ta[:, hs], func=ACT.Square)
+            for hs in parts:
                 nc.vector.tensor_scalar_max(out=tsq[:, hs], in0=tsq[:, hs], scalar1=CUT * CUT)
+            for hs in parts:
                 nc.vector.scalar_tensor_tensor(
                     out=ta[:, hs], in0=tsq[:, hs], scalar=1.0, in1=tsq[:, hs], op0=ALU.add, op1=ALU.mult)
             nc.scalar.activation(out=tb[:, al], in_=tb[:, al], func=ACT.Tanh, scale=1.0 / RT2)
@@ -248,11 +282,25 @@ def tile_hyperboliclayer_t_kernel(tc, z, p, normals, out):
             tb = ep1.tile([P, PIX], F32, name="tb")
             tsq = ep2.tile([P, PIX], F32, name="tsq")
             cuts = (0, PIX) if more else LAST_CUTS
+            front_y(r, 0)
+            front_y(r, 1)
+            front_q(r, 0)
+            front_mx(r, 0, ta)
             for lo, hi in zip(cuts[:-1], cuts[1:]):
                 for i in range(lo // SUB, hi // SUB):
-                    front(r, i, ta, tb)
+                    if i + 2 < PIX // SUB:
+                        front_y(r, i + 2)
+                    front_e1(r, i, ta, tb)
+                    if i + 1 < PIX // SUB:
+                        front_q(r, i + 1)
+                    front_e2(r, i, ta)
                     if more:
-                        norm_blocks(r + 1, 4 * i, 4 * i + 4)
+                        norm_blocks(r + 1, 4 * i, 4 * i + 2)
+                    front_e3(r, i, ta)
+                    if i + 1 < PIX // SUB:
+                        front_mx(r, i + 1, ta)
+                    if more:
+                        norm_blocks(r + 1, 4 * i + 2, 4 * i + 4)
                 if more:
                     norm_chain(r + 1, 0, NBLK)
                 if r + 2 < BATCH:

@@ -84,8 +84,8 @@ def tile_hyperboliclayer_t_kernel(tc, z, p, normals, out):
         nc.vector.tensor_scalar(out=c_2b[:], in0=pp[:], scalar1=-2.0, scalar2=2.0, op0=ALU.mult, op1=ALU.add)
         c_1pp = const.tile([P, 1], F32)
         nc.vector.tensor_scalar(out=c_1pp[:], in0=pp[:], scalar1=1.0, scalar2=None, op0=ALU.add)
-        c_mpp = const.tile([P, 1], F32)
-        nc.vector.tensor_scalar(out=c_mpp[:], in0=pp[:], scalar1=-1.0, scalar2=None, op0=ALU.mult)
+        c_mepp = const.tile([P, 1], F32)
+        nc.vector.tensor_scalar(out=c_mepp[:], in0=pp[:], scalar1=-EPS, scalar2=None, op0=ALU.mult)
         c_b = const.tile([P, 1], F32)
         nc.vector.tensor_scalar(out=c_b[:], in0=pp[:], scalar1=-1.0, scalar2=1.0, op0=ALU.mult, op1=ALU.add)
         c_2pwb = const.tile([P, 1], F32)
@@ -116,7 +116,7 @@ def tile_hyperboliclayer_t_kernel(tc, z, p, normals, out):
 
         NBLK = PIX // BLK
 
-        NAMES = ("s", "r0", "nw", "rn", "n", "th", "e", "f", "d", "rd", "g", "h")
+        NAMES = ("s", "r0", "nw", "rn", "n", "th", "e", "f", "d", "re", "h")
         per_pixel = {}
 
         def norm_tiles(r):
@@ -151,10 +151,10 @@ def tile_hyperboliclayer_t_kernel(tc, z, p, normals, out):
             nc.scalar.activation(out=v["e"], in_=v["n"], func=ACT.Exp, scale=-2.0)
             nc.vector.tensor_tensor(out=v["f"], in0=v["th"], in1=v["rn"], op=ALU.mult)
             nc.vector.tensor_scalar(out=v["d"], in0=v["e"], scalar1=1.0, scalar2=None, op0=ALU.add)
-            nc.vector.reciprocal(out=v["rd"], in_=v["d"])
-            nc.vector.scalar_tensor_tensor(out=v["g"], in0=v["e"], scalar=4.0, in1=v["rd"], op0=ALU.mult, op1=ALU.mult)
-            nc.vector.tensor_tensor(out=v["g"], in0=v["g"], in1=v["rd"], op=ALU.mult)
-            nc.vector.reciprocal(out=v["h"], in_=v["g"])
+            nc.vector.tensor_scalar_max(out=v["e"], in0=v["e"], scalar1=1e-30)
+            nc.vector.reciprocal(out=v["re"], in_=v["e"])
+            nc.vector.tensor_tensor(out=v["d"], in0=v["d"], in1=v["d"], op=ALU.mult)
+            nc.vector.scalar_tensor_tensor(out=v["h"], in0=v["d"], scalar=0.25, in1=v["re"], op0=ALU.mult, op1=ALU.mult)
 
         def spread(dst, col_tile, first_blk):
             for j in range(SUB // BLK):
@@ -163,100 +163,59 @@ def tile_hyperboliclayer_t_kernel(tc, z, p, normals, out):
                     dst[:, j * BLK : (j + 1) * BLK], col_tile[:, b : b + 1].to_broadcast([P, P]), ident_f[:]
                 )
 
-        ygs = {}
-        banks = {}
-
-        def front_y(r, i):
+        def front(r, i, ta, tb):
+            f, h = per_pixel[r]["f"], per_pixel[r]["h"]
+            z_sb = z_tiles[r]
             cs = slice(i * SUB, (i + 1) * SUB)
             fb = ps_fb.tile([P, SUB], F32, name="fb")
-            spread(fb, per_pixel[r]["f"], 4 * i)
+            spread(fb, f, 4 * i)
             yg = ypool.tile([P, SUB, PACK], BF16, align_bytes=64, name="yg")
             nc.vector.tensor_tensor(
-                out=yg[:], in0=z_tiles[r][:, :, cs].rearrange("p t w -> p w t"),
+                out=yg[:], in0=z_sb[:, :, cs].rearrange("p t w -> p w t"),
                 in1=fb[:].unsqueeze(2).to_broadcast([P, SUB, PACK]), op=ALU.mult,
             )
-            ygs[(r, i)] = yg
-
-        def front_q(r, i):
             codes = ypool.tile([P, SUB], U32, align_bytes=64, name="codes")
             scale = ypool.tile([P, SUB], U8, align_bytes=64, name="scale")
             nc.vector.quantize_mx(
-                out=codes[:].bitcast(FP8X4), scales=scale[:], in_=ygs[(r, i)][:].rearrange("p w t -> p (w t)")
+                out=codes[:].bitcast(FP8X4), scales=scale[:], in_=yg[:].rearrange("p w t -> p (w t)")
             )
-            banks[(r, i)] = (codes, scale)
-
-        def front_mx(r, i, ta):
-            cs = slice(i * SUB, (i + 1) * SUB)
-            codes, scale = banks[(r, i)]
             a_ps = ps_ep.tile([P, SUB], F32, name="a_ps")
             nc.tensor.matmul_mx(
                 out=a_ps[:], lhsT=wcodes[:, 0:P].bitcast(FP8X4), lhsT_scale=wscale[:, 0:P],
                 rhs=codes[:].bitcast(FP8X4), rhs_scale=scale[:], start=True, stop=True,
             )
-            w_ps = ps_ep.tile([P, SUB], F32, name="w_ps")
+            w_ps = ps_ep.tile([P, SUB], F32, name="w_ps", bufs=2)
             nc.tensor.matmul_mx(
                 out=w_ps[:], lhsT=wcodes[:, P : 2 * P].bitcast(FP8X4), lhsT_scale=wscale[:, P : 2 * P],
                 rhs=codes[:].bitcast(FP8X4), rhs_scale=scale[:], start=True, stop=True,
             )
-            gb = ps_ep.tile([P, SUB], F32, name="gb")
-            spread(gb, per_pixel[r]["g"], 4 * i)
+            hb = ps_ep.tile([P, SUB], F32, name="hb")
+            spread(hb, h, 4 * i)
             nc.scalar.activation(out=ta[:, cs], in_=a_ps[:], func=ACT.Identity, scale=2.0, bias=c_1pp[:])
-            banks[(r, i)] = (w_ps, gb)
-
-        def front_e1(r, i, ta, tb):
-            cs = slice(i * SUB, (i + 1) * SUB)
-            gb = banks[(r, i)][1]
-            nc.vector.scalar_tensor_tensor(
-                out=tb[:, cs], in0=gb[:], scalar=c_mpp[:], in1=ta[:, cs], op0=ALU.mult, op1=ALU.add)
+            nc.vector.tensor_tensor(out=tb[:, cs], in0=ta[:, cs], in1=hb[:], op=ALU.mult)
             nc.vector.tensor_scalar(
                 out=ta[:, cs], in0=ta[:, cs], scalar1=c_2pw[:], scalar2=c_2pwb[:], op0=ALU.mult, op1=ALU.add)
-
-        def front_e2(r, i, ta):
-            cs = slice(i * SUB, (i + 1) * SUB)
             nc.vector.scalar_tensor_tensor(
-                out=ta[:, cs], in0=banks[(r, i)][1][:], scalar=c_m2pw[:], in1=ta[:, cs], op0=ALU.mult, op1=ALU.add)
-
-        def front_e3(r, i, ta):
-            cs = slice(i * SUB, (i + 1) * SUB)
-            nc.vector.scalar_tensor_tensor(
-                out=ta[:, cs], in0=banks[(r, i)][0][:], scalar=c_2b[:], in1=ta[:, cs], op0=ALU.mult, op1=ALU.add)
+                out=ta[:, cs], in0=w_ps[:], scalar=c_2b[:], in1=ta[:, cs], op0=ALU.mult, op1=ALU.add)
+            nc.vector.tensor_tensor(out=ta[:, cs], in0=ta[:, cs], in1=hb[:], op=ALU.mult)
 
         def back(r, ta, tb, tsq, lo, hi):
-            h = per_pixel[r]["h"]
             al = slice(lo, hi)
             piece = min(HALF, hi - lo)
             parts = [slice(c0, c0 + piece) for c0 in range(lo, hi, piece)]
-            nc.scalar.activation(out=tb[:, al], in_=tb[:, al], func=ACT.Abs_reciprocal_sqrt, scale=EPS)
+            nc.scalar.activation(out=tb[:, al], in_=tb[:, al], func=ACT.Abs_reciprocal_sqrt, scale=EPS, bias=c_mepp[:])
             nc.scalar.activation(out=tb[:, al], in_=tb[:, al], func=ACT.Square)
-            def limit(i):
-                cs = slice(i * SUB, (i + 1) * SUB)
-                hb = ps_ep.tile([P, SUB], F32, name="hb")
-                spread(hb, h, 4 * i)
+            for q0 in range(lo, hi, QUART):
+                qs = slice(q0, q0 + QUART)
+                nc.vector.tensor_scalar(out=tb[:, qs], in0=tb[:, qs], scalar1=c_i1[:], scalar2=None, op0=ALU.min)
                 nc.vector.scalar_tensor_tensor(
-                    out=tb[:, cs], in0=hb[:], scalar=c_i1[:], in1=tb[:, cs], op0=ALU.mult, op1=ALU.min)
-
-            def clamp(qs):
+                    out=ta[:, qs], in0=ta[:, qs], scalar=c_m2pw[:], in1=tb[:, qs], op0=ALU.add, op1=ALU.mult)
                 nc.vector.tensor_scalar(
                     out=tb[:, qs], in0=ta[:, qs], scalar1=-CUT, scalar2=CUT, op0=ALU.max, op1=ALU.min)
                 nc.vector.tensor_scalar_min(out=ta[:, qs], in0=ta[:, qs], scalar1=85.0)
-
-            quarts = [slice(q0, q0 + QUART) for q0 in range(lo, hi, QUART)]
-            first = lo // SUB
-            limit(first)
-            limit(first + 1)
-            for n, qs in enumerate(quarts):
-                if n + 1 < len(quarts):
-                    limit(first + 2 * n + 2)
-                    limit(first + 2 * n + 3)
-                nc.vector.tensor_tensor(out=ta[:, qs], in0=ta[:, qs], in1=tb[:, qs], op=ALU.mult)
-                if n > 0:
-                    clamp(quarts[n - 1])
-            clamp(quarts[-1])
             for hs in parts:
                 nc.scalar.activation(out=tsq[:, hs], in_=ta[:, hs], func=ACT.Square)
-            for hs in parts:
                 nc.vector.tensor_scalar_max(out=tsq[:, hs], in0=tsq[:, hs], scalar1=CUT * CUT)
-            for hs in parts:
                 nc.vector.scalar_tensor_tensor(
                     out=ta[:, hs], in0=tsq[:, hs], scalar=1.0, in1=tsq[:, hs], op0=ALU.add, op1=ALU.mult)
             nc.scalar.activation(out=tb[:, al], in_=tb[:, al], func=ACT.Tanh, scale=1.0 / RT2)
@@ -282,25 +241,11 @@ def tile_hyperboliclayer_t_kernel(tc, z, p, normals, out):
             tb = ep1.tile([P, PIX], F32, name="tb")
             tsq = ep2.tile([P, PIX], F32, name="tsq")
             cuts = (0, PIX) if more else LAST_CUTS
-            front_y(r, 0)
-            front_y(r, 1)
-            front_q(r, 0)
-            front_mx(r, 0, ta)
             for lo, hi in zip(cuts[:-1], cuts[1:]):
                 for i in range(lo // SUB, hi // SUB):
-                    if i + 2 < PIX // SUB:
-                        front_y(r, i + 2)
-                    front_e1(r, i, ta, tb)
-                    if i + 1 < PIX // SUB:
-                        front_q(r, i + 1)
-                    front_e2(r, i, ta)
+                    front(r, i, ta, tb)
                     if more:
-                        norm_blocks(r + 1, 4 * i, 4 * i + 2)
-                    front_e3(r, i, ta)
-                    if i + 1 < PIX // SUB:
-                        front_mx(r, i + 1, ta)
-                    if more:
-                        norm_blocks(r + 1, 4 * i + 2, 4 * i + 4)
+                        norm_blocks(r + 1, 4 * i, 4 * i + 4)
                 if more:
                     norm_chain(r + 1, 0, NBLK)
                 if r + 2 < BATCH:

@@ -76,8 +76,8 @@ def tile_hyperboliclayer_t_kernel(tc, z, p, normals, out):
         nc.vector.tensor_tensor(out=prod[:], in0=p_sb[:], in1=n_sb[:], op=ALU.mult)
         spn = const.tile([P, 1], F32)
         nc.vector.reduce_sum(out=spn[:], in_=prod[:], axis=AX.X)
-        c_2pw = const.tile([P, 1], F32)
-        nc.vector.tensor_scalar(out=c_2pw[:], in0=spn[:], scalar1=-2.0, scalar2=None, op0=ALU.mult)
+        c_4pw = const.tile([P, 1], F32)
+        nc.vector.tensor_scalar(out=c_4pw[:], in0=spn[:], scalar1=-4.0, scalar2=None, op0=ALU.mult)
         c_m2pw = const.tile([P, 1], F32)
         nc.vector.tensor_scalar(out=c_m2pw[:], in0=spn[:], scalar1=2.0, scalar2=None, op0=ALU.mult)
         c_2b = const.tile([P, 1], F32)
@@ -88,8 +88,6 @@ def tile_hyperboliclayer_t_kernel(tc, z, p, normals, out):
         nc.vector.tensor_scalar(out=c_mepp[:], in0=pp[:], scalar1=-EPS, scalar2=None, op0=ALU.mult)
         c_b = const.tile([P, 1], F32)
         nc.vector.tensor_scalar(out=c_b[:], in0=pp[:], scalar1=-1.0, scalar2=1.0, op0=ALU.mult, op1=ALU.add)
-        c_2pwb = const.tile([P, 1], F32)
-        nc.vector.tensor_tensor(out=c_2pwb[:], in0=c_2pw[:], in1=c_b[:], op=ALU.mult)
         c_1 = const.tile([P, 1], F32)
         nc.vector.tensor_tensor(out=c_1[:], in0=c_b[:], in1=ww[:], op=ALU.mult)
         c_i1 = const.tile([P, 1], F32)
@@ -191,10 +189,9 @@ def tile_hyperboliclayer_t_kernel(tc, z, p, normals, out):
             )
             hb = ps_ep.tile([P, SUB], F32, name="hb")
             spread(hb, h, 4 * i)
-            nc.scalar.activation(out=ta[:, cs], in_=a_ps[:], func=ACT.Identity, scale=2.0, bias=c_1pp[:])
-            nc.vector.tensor_tensor(out=tb[:, cs], in0=ta[:, cs], in1=hb[:], op=ALU.mult)
-            nc.vector.tensor_scalar(
-                out=ta[:, cs], in0=ta[:, cs], scalar1=c_2pw[:], scalar2=c_2pwb[:], op0=ALU.mult, op1=ALU.add)
+            nc.scalar.activation(out=tb[:, cs], in_=a_ps[:], func=ACT.Identity, scale=2.0, bias=c_1pp[:])
+            nc.scalar.activation(out=ta[:, cs], in_=a_ps[:], func=ACT.Identity, scale=c_4pw[:], bias=c_4pw[:])
+            nc.vector.tensor_tensor(out=tb[:, cs], in0=tb[:, cs], in1=hb[:], op=ALU.mult)
             nc.vector.scalar_tensor_tensor(
                 out=ta[:, cs], in0=w_ps[:], scalar=c_2b[:], in1=ta[:, cs], op0=ALU.mult, op1=ALU.add)
             nc.vector.tensor_tensor(out=ta[:, cs], in0=ta[:, cs], in1=hb[:], op=ALU.mult)

@@ -24,6 +24,7 @@ QUART = 1024
 FIRST_BATCHES = (0, 8, 16, 32)
 LAST_CUTS = (0, 2048, 3072, 4096)
 BLK = 128
+NORMS_DONE = (0, 6, 12, 18, 24, 30, 32, 32, 32)
 EPS = 1e-5
 CUT = 0.005
 RT2 = 2.0 ** 0.5
@@ -242,9 +243,9 @@ def tile_hyperboliclayer_t_kernel(tc, z, p, normals, out):
                 for i in range(lo // SUB, hi // SUB):
                     front(r, i, ta, tb)
                     if more:
-                        norm_blocks(r + 1, 4 * i, 4 * i + 4)
-                if more:
-                    norm_chain(r + 1, 0, NBLK)
+                        norm_blocks(r + 1, NORMS_DONE[i], NORMS_DONE[i + 1])
+                        if NORMS_DONE[i] < NBLK and NORMS_DONE[i + 1] == NBLK:
+                            norm_chain(r + 1, 0, NBLK)
                 if r + 2 < BATCH:
                     load_z(r + 2, 1)
                 back(r, ta, tb, tsq, lo, hi)

@@ -21,7 +21,7 @@ PIX = 4096
 SUB = 512
 HALF = 2048
 QUART = 1024
-FIRST_BATCHES = (0, 8, 16, 32)
+FIRST_BATCHES = (0, 16, 32)
 LAST_CUTS = (0, 2048, 3072, 4096)
 BLK = 128
 NORMS_DONE = (0, 6, 12, 18, 24, 30, 32, 32, 32)

from contextlib import ExitStack

import concourse.mybir as mybir
from concourse.masks import make_identity

FLOPS = 2 * 2 * 128 * 512 * 4 * 4096

F32 = mybir.dt.float32
BF16 = mybir.dt.bfloat16
U32 = mybir.dt.uint32
U8 = mybir.dt.uint8
FP8X4 = mybir.dt.float8_e4m3fn_x4
ALU = mybir.AluOpType
ACT = mybir.ActivationFunctionType
AX = mybir.AxisListType

P = 128
PACK = 4
BATCH = 4
PIX = 4096
SUB = 512
HALF = 2048
QUART = 1024
FIRST_BATCHES = (0, 16, 32)
LAST_CUTS = (0, 2048, 3072, 4096)
BLK = 128
NORMS_DONE = (0, 6, 12, 18, 24, 30, 32, 32, 32)
EPS = 1e-5
CUT = 0.005
RT2 = 2.0 ** 0.5
XC = CUT / RT2
TANH_XC = XC - XC ** 3 / 3.0 + 2.0 * XC ** 5 / 15.0


def tile_hyperboliclayer_t_kernel(tc, z, p, normals, out):
    nc = tc.nc
    with ExitStack() as ctx:
        const = ctx.enter_context(tc.tile_pool(name="const", bufs=1))
        zpool = ctx.enter_context(tc.tile_pool(name="zpool", bufs=2))
        ypool = ctx.enter_context(tc.tile_pool(name="ypool", bufs=3))
        small = ctx.enter_context(tc.tile_pool(name="small", bufs=2))
        ep1 = ctx.enter_context(tc.tile_pool(name="ep1", bufs=2))
        ep2 = ctx.enter_context(tc.tile_pool(name="ep2", bufs=2))
        ps_zt = ctx.enter_context(tc.psum_pool(name="ps_zt", bufs=2))
        ps_fb = ctx.enter_context(tc.psum_pool(name="ps_fb", bufs=2))
        ps_ep = ctx.enter_context(tc.psum_pool(name="ps_ep", bufs=1))

        ident_bf = const.tile([P, P], BF16)
        make_identity(nc, ident_bf[:])
        ident_f = const.tile([P, P], F32)
        make_identity(nc, ident_f[:])

        p_sb = const.tile([P, 512], BF16)
        nc.sync.dma_start(out=p_sb[:], in_=p)
        n_sb = const.tile([P, 512], BF16)
        nc.sync.dma_start(out=n_sb[:], in_=normals)

        z_tiles = []

        def load_z(r, pieces):
            z_sb = zpool.tile([P, PACK, PIX], BF16, name="z_sb")
            src = z[r].rearrange("(q t) h w -> q t (h w)", t=PACK)
            step = PIX // pieces
            for c in range(pieces):
                nc.sync.dma_start(out=z_sb[:, :, c * step : (c + 1) * step], in_=src[:, :, c * step : (c + 1) * step])
            z_tiles.append(z_sb)

        load_z(0, 4)
        load_z(1, 1)

        junk_c = const.tile([P, 512], F32)
        pp = const.tile([P, 1], F32)
        nc.scalar.activation(out=junk_c[:], in_=p_sb[:], func=ACT.Square, accum_out=pp[:])
        ww = const.tile([P, 1], F32)
        nc.scalar.activation(out=junk_c[:], in_=n_sb[:], func=ACT.Square, accum_out=ww[:])
        prod = const.tile([P, 512], F32)
        nc.vector.tensor_tensor(out=prod[:], in0=p_sb[:], in1=n_sb[:], op=ALU.mult)
        spn = const.tile([P, 1], F32)
        nc.vector.reduce_sum(out=spn[:], in_=prod[:], axis=AX.X)
        c_4pw = const.tile([P, 1], F32)
        nc.vector.tensor_scalar(out=c_4pw[:], in0=spn[:], scalar1=-4.0, scalar2=None, op0=ALU.mult)
        c_m2pw = const.tile([P, 1], F32)
        nc.vector.tensor_scalar(out=c_m2pw[:], in0=spn[:], scalar1=2.0, scalar2=None, op0=ALU.mult)
        c_2b = const.tile([P, 1], F32)
        nc.vector.tensor_scalar(out=c_2b[:], in0=pp[:], scalar1=-2.0, scalar2=2.0, op0=ALU.mult, op1=ALU.add)
        c_1pp = const.tile([P, 1], F32)
        nc.vector.tensor_scalar(out=c_1pp[:], in0=pp[:], scalar1=1.0, scalar2=None, op0=ALU.add)
        c_mepp = const.tile([P, 1], F32)
        nc.vector.tensor_scalar(out=c_mepp[:], in0=pp[:], scalar1=-EPS, scalar2=None, op0=ALU.mult)
        c_b = const.tile([P, 1], F32)
        nc.vector.tensor_scalar(out=c_b[:], in0=pp[:], scalar1=-1.0, scalar2=1.0, op0=ALU.mult, op1=ALU.add)
        c_1 = const.tile([P, 1], F32)
        nc.vector.tensor_tensor(out=c_1[:], in0=c_b[:], in1=ww[:], op=ALU.mult)
        c_i1 = const.tile([P, 1], F32)
        nc.vector.reciprocal(out=c_i1[:], in_=c_1[:])
        c_out = const.tile([P, 1], F32)
        nc.vector.tensor_scalar(out=c_out[:], in0=ww[:], scalar1=-1.0 / TANH_XC, scalar2=None, op0=ALU.mult)

        wg = const.tile([P, 2 * PACK, P], BF16)
        nc.vector.tensor_scalar(
            out=wg[:, 0:PACK, :], in0=p_sb[:].rearrange("c (q t) -> c t q", t=PACK),
            scalar1=-1.0, scalar2=None, op0=ALU.mult,
        )
        nc.vector.tensor_copy(out=wg[:, PACK : 2 * PACK, :], in_=n_sb[:].rearrange("c (q t) -> c t q", t=PACK))
        wt_ps = ps_zt.tile([P, 2 * PACK, P], BF16, tag="zt")
        for j in range(2 * PACK):
            nc.tensor.transpose(wt_ps[:, j, :], wg[:, j, :], ident_bf[:])
        wgrp = const.tile([P, 2, P, PACK], BF16, align_bytes=64)
        nc.vector.tensor_copy(out=wgrp[:], in_=wt_ps[:].rearrange("q (o t) c -> q o c t", o=2))
        wcodes = const.tile([P, 2 * P], U32, align_bytes=64)
        wscale = const.tile([P, 2 * P], U8, align_bytes=64)
        nc.vector.quantize_mx(
            out=wcodes[:].bitcast(FP8X4), scales=wscale[:], in_=wgrp[:].rearrange("q o c t -> q (o c t)")
        )

        NBLK = PIX // BLK

        NAMES = ("s", "r0", "nw", "rn", "n", "th", "e", "f", "d", "re", "h")
        per_pixel = {}

        def norm_tiles(r):
            per_pixel[r] = dict((nm, small.tile([P, NBLK], F32, name=nm)) for nm in NAMES)

        def norm_blocks(r, c0, c1):
            z_sb = z_tiles[r]
            for b2 in range(c0 // 2, c1 // 2):
                zt = ps_zt.tile([P, 2, PACK, P], BF16, tag="zt", name="zt")
                for u in range(2):
                    blk = 2 * b2 + u
                    for k in range(PACK):
                        nc.tensor.transpose(zt[:, u, k, :], z_sb[:, k, blk * BLK : (blk + 1) * BLK], ident_bf[:])
                for u in range(2):
                    blk = 2 * b2 + u
                    junk = small.tile([P, PACK * P], BF16, name="junk")
                    nc.scalar.activation(
                        out=junk[:], in_=zt[:, u, :, :].rearrange("p t q -> p (t q)"), func=ACT.Square,
                        accum_out=per_pixel[r]["s"][:, blk : blk + 1],
                    )

        def norm_chain(r, c0, c1):
            v = dict((nm, per_pixel[r][nm][:, c0:c1]) for nm in NAMES)
            nc.vector.tensor_scalar_max(out=v["s"], in0=v["s"], scalar1=1e-30)
            nc.scalar.activation(out=v["r0"], in_=v["s"], func=ACT.Abs_reciprocal_sqrt)
            nc.vector.tensor_tensor(out=v["nw"], in0=v["r0"], in1=v["r0"], op=ALU.mult)
            nc.vector.tensor_tensor(out=v["nw"], in0=v["nw"], in1=v["s"], op=ALU.mult)
            nc.vector.tensor_scalar(out=v["nw"], in0=v["nw"], scalar1=-0.5, scalar2=1.5, op0=ALU.mult, op1=ALU.add)
            nc.vector.tensor_tensor(out=v["rn"], in0=v["r0"], in1=v["nw"], op=ALU.mult)
            nc.vector.tensor_tensor(out=v["n"], in0=v["s"], in1=v["rn"], op=ALU.mult)
            nc.scalar.activation(out=v["th"], in_=v["n"], func=ACT.Tanh)
            nc.scalar.activation(out=v["e"], in_=v["n"], func=ACT.Exp, scale=-2.0)
            nc.vector.tensor_tensor(out=v["f"], in0=v["th"], in1=v["rn"], op=ALU.mult)
            nc.vector.tensor_scalar(out=v["d"], in0=v["e"], scalar1=1.0, scalar2=None, op0=ALU.add)
            nc.vector.tensor_scalar_max(out=v["e"], in0=v["e"], scalar1=1e-30)
            nc.vector.reciprocal(out=v["re"], in_=v["e"])
            nc.vector.tensor_tensor(out=v["d"], in0=v["d"], in1=v["d"], op=ALU.mult)
            nc.vector.scalar_tensor_tensor(out=v["h"], in0=v["d"], scalar=0.25, in1=v["re"], op0=ALU.mult, op1=ALU.mult)

        def spread(dst, col_tile, first_blk):
            for j in range(SUB // BLK):
                b = first_blk + j
                nc.tensor.transpose(
                    dst[:, j * BLK : (j + 1) * BLK], col_tile[:, b : b + 1].to_broadcast([P, P]), ident_f[:]
                )

        def front(r, i, ta, tb):
            f, h = per_pixel[r]["f"], per_pixel[r]["h"]
            z_sb = z_tiles[r]
            cs = slice(i * SUB, (i + 1) * SUB)
            fb = ps_fb.tile([P, SUB], F32, name="fb")
            spread(fb, f, 4 * i)
            yg = ypool.tile([P, SUB, PACK], BF16, align_bytes=64, name="yg")
            nc.vector.tensor_tensor(
                out=yg[:], in0=z_sb[:, :, cs].rearrange("p t w -> p w t"),
                in1=fb[:].unsqueeze(2).to_broadcast([P, SUB, PACK]), op=ALU.mult,
            )
            codes = ypool.tile([P, SUB], U32, align_bytes=64, name="codes")
            scale = ypool.tile([P, SUB], U8, align_bytes=64, name="scale")
            nc.vector.quantize_mx(
                out=codes[:].bitcast(FP8X4), scales=scale[:], in_=yg[:].rearrange("p w t -> p (w t)")
            )
            a_ps = ps_ep.tile([P, SUB], F32, name="a_ps")
            nc.tensor.matmul_mx(
                out=a_ps[:], lhsT=wcodes[:, 0:P].bitcast(FP8X4), lhsT_scale=wscale[:, 0:P],
                rhs=codes[:].bitcast(FP8X4), rhs_scale=scale[:], start=True, stop=True,
            )
            w_ps = ps_ep.tile([P, SUB], F32, name="w_ps", bufs=2)
            nc.tensor.matmul_mx(
                out=w_ps[:], lhsT=wcodes[:, P : 2 * P].bitcast(FP8X4), lhsT_scale=wscale[:, P : 2 * P],
                rhs=codes[:].bitcast(FP8X4), rhs_scale=scale[:], start=True, stop=True,
            )
            hb = ps_ep.tile([P, SUB], F32, name="hb")
            spread(hb, h, 4 * i)
            nc.scalar.activation(out=tb[:, cs], in_=a_ps[:], func=ACT.Identity, scale=2.0, bias=c_1pp[:])
            nc.scalar.activation(out=ta[:, cs], in_=a_ps[:], func=ACT.Identity, scale=c_4pw[:], bias=c_4pw[:])
            nc.vector.tensor_tensor(out=tb[:, cs], in0=tb[:, cs], in1=hb[:], op=ALU.mult)
            nc.vector.scalar_tensor_tensor(
                out=ta[:, cs], in0=w_ps[:], scalar=c_2b[:], in1=ta[:, cs], op0=ALU.mult, op1=ALU.add)
            nc.vector.tensor_tensor(out=ta[:, cs], in0=ta[:, cs], in1=hb[:], op=ALU.mult)

        def back(r, ta, tb, tsq, lo, hi):
            al = slice(lo, hi)
            piece = min(HALF, hi - lo)
            parts = [slice(c0, c0 + piece) for c0 in range(lo, hi, piece)]
            nc.scalar.activation(out=tb[:, al], in_=tb[:, al], func=ACT.Abs_reciprocal_sqrt, scale=EPS, bias=c_mepp[:])
            nc.scalar.activation(out=tb[:, al], in_=tb[:, al], func=ACT.Square)
            for q0 in range(lo, hi, QUART):
                qs = slice(q0, q0 + QUART)
                nc.vector.tensor_scalar(out=tb[:, qs], in0=tb[:, qs], scalar1=c_i1[:], scalar2=None, op0=ALU.min)
                nc.vector.scalar_tensor_tensor(
                    out=ta[:, qs], in0=ta[:, qs], scalar=c_m2pw[:], in1=tb[:, qs], op0=ALU.add, op1=ALU.mult)
                nc.vector.tensor_scalar(
                    out=tb[:, qs], in0=ta[:, qs], scalar1=-CUT, scalar2=CUT, op0=ALU.max, op1=ALU.min)
                nc.vector.tensor_scalar_min(out=ta[:, qs], in0=ta[:, qs], scalar1=85.0)
            for hs in parts:
                nc.scalar.activation(out=tsq[:, hs], in_=ta[:, hs], func=ACT.Square)
                nc.vector.tensor_scalar_max(out=tsq[:, hs], in0=tsq[:, hs], scalar1=CUT * CUT)
                nc.vector.scalar_tensor_tensor(
                    out=ta[:, hs], in0=tsq[:, hs], scalar=1.0, in1=tsq[:, hs], op0=ALU.add, op1=ALU.mult)
            nc.scalar.activation(out=tb[:, al], in_=tb[:, al], func=ACT.Tanh, scale=1.0 / RT2)
            nc.scalar.activation(out=ta[:, al], in_=ta[:, al], func=ACT.Sqrt, scale=4.0)
            for hs in parts:
                nc.vector.scalar_tensor_tensor(
                    out=ta[:, hs], in0=tsq[:, hs], scalar=2.0, in1=ta[:, hs], op0=ALU.mult, op1=ALU.add)
            nc.scalar.activation(out=ta[:, al], in_=ta[:, al], func=ACT.Ln, bias=1.0)
            for hs in parts:
                nc.vector.scalar_tensor_tensor(
                    out=ta[:, hs], in0=ta[:, hs], scalar=c_out[:], in1=tb[:, hs], op0=ALU.mult, op1=ALU.mult)
                nc.sync.dma_start(out=out[r].rearrange("k h w -> k (h w)")[:, hs], in_=ta[:, hs])

        norm_tiles(0)
        for c0, c1 in zip(FIRST_BATCHES[:-1], FIRST_BATCHES[1:]):
            norm_blocks(0, c0, c1)
            norm_chain(0, c0, c1)
        for r in range(BATCH):
            more = r + 1 < BATCH
            if more:
                norm_tiles(r + 1)
            ta = ep1.tile([P, PIX], F32, name="ta")
            tb = ep1.tile([P, PIX], F32, name="tb")
            tsq = ep2.tile([P, PIX], F32, name="tsq")
            cuts = (0, PIX) if more else LAST_CUTS
            for lo, hi in zip(cuts[:-1], cuts[1:]):
                for i in range(lo // SUB, hi // SUB):
                    front(r, i, ta, tb)
                    if more:
                        norm_blocks(r + 1, NORMS_DONE[i], NORMS_DONE[i + 1])
                        if NORMS_DONE[i] < NBLK and NORMS_DONE[i + 1] == NBLK:
                            norm_chain(r + 1, 0, NBLK)
                if r + 2 < BATCH:
                    load_z(r + 2, 1)
                back(r, ta, tb, tsq, lo, hi)
